import numpy as np
import ml_dtypes


def mxq(x, axis, fmt="e4m3"):
    dtype, down = {"e4m3": (ml_dtypes.float8_e4m3fn, 7), "e5m2": (ml_dtypes.float8_e5m2, 14)}[fmt]
    v = np.moveaxis(np.asarray(x, np.float32).astype(ml_dtypes.bfloat16).astype(np.float64), axis, -1)
    blocks = v.reshape(v.shape[:-1] + (-1, 32))
    amax = np.abs(blocks).max(-1, keepdims=True)
    byte = np.maximum(np.where(amax > 0, np.frexp(amax)[1] - 1 + 127, 0) - down, 1)
    scale = np.exp2(byte - 127.0)
    codes = (blocks / scale).astype(np.float32).astype(dtype).astype(np.float64)
    return np.moveaxis((codes * scale).reshape(v.shape), -1, axis)


WIDE = False


def mx_kscale(k):
    if not WIDE:
        return np.ones(k)
    levels = np.array([10, -10, 5, -5, 0])
    if k % 512:
        return np.exp2(np.random.permutation(np.resize(levels, k // 32))).repeat(32)
    a = np.empty((k // 512, 16))
    for p in range(k // 512):
        a[p, :8] = np.random.permutation(np.resize(levels, 8))
        for g in range(8):
            far = levels[np.abs(levels - a[p, g]) >= 10]
            a[p, g + 8] = far[np.random.randint(len(far))]
    return np.exp2(a.ravel()).repeat(32)


BF16 = ml_dtypes.bfloat16


def bf(x):
    return np.asarray(x, np.float32).astype(BF16)


def f64(x):
    return np.asarray(x).astype(np.float64)


B, S, D_MODEL, H, NOPE, ROPE = 1, 512, 2048, 4, 256, 128
DK = D_MODEL // H
LAT = 3 * DK
D_HEAD = NOPE + ROPE
D_LATENT = H * D_HEAD
ROT_DIM = 2 * ((ROPE // 2) // 2)
EPS = 1e-6


def rmsnorm(x, w):
    return x * (1.0 / np.sqrt(np.mean(x * x, axis=-1, keepdims=True) + EPS)) * w


def apply_rope(x):
    inv_freq = 1.0 / (10000.0 ** (np.arange(0, ROT_DIM, 2) / ROT_DIM))
    freqs = np.arange(x.shape[-2])[:, None] * inv_freq[None, :]
    freqs = np.repeat(freqs, 2, axis=-1)
    cos, sin = np.cos(freqs), np.sin(freqs)
    xl, xr = x[..., :ROT_DIM], x[..., ROT_DIM:]
    x1, x2 = xl[..., 0::2], xl[..., 1::2]
    rot = np.stack([-x2, x1], axis=-1).reshape(xl.shape)
    return np.concatenate([xl * cos + rot * sin, xr], axis=-1)


def to_heads(t):
    return t.reshape(B, S, D_HEAD, H).transpose(0, 3, 1, 2)


def draw0():
    s, t = mx_kscale(D_MODEL), mx_kscale(LAT)
    return {"x": bf(np.random.standard_normal((B, S, D_MODEL)) * s),
            "w_down": bf(np.random.standard_normal((D_MODEL, LAT)) / np.sqrt(D_MODEL) / s[:, None]),
            "rms_w": bf((1.0 + 0.1 * np.random.standard_normal(LAT)) * t),
            "w_up": bf(np.random.standard_normal((LAT, 3 * D_LATENT)) * 1.25 / np.sqrt(LAT) / t[:, None])}


def core(x, w_down, rms_w, w_up):
    h = mxq(f64(x), 2, "e4m3") @ mxq(f64(w_down), 0, "e4m3")
    h = rmsnorm(h, f64(rms_w))
    qkv = mxq(h, 2, "e4m3") @ mxq(f64(w_up), 0, "e4m3")
    q, k, v = np.split(qkv, 3, axis=-1)
    q, k, v = to_heads(q), to_heads(k), to_heads(v)
    q_nope, q_rope = q[..., :NOPE], q[..., NOPE:]
    k_nope, k_rope = k[..., :NOPE], k[..., NOPE:]
    q_rope = apply_rope(q_rope)
    k_rope = apply_rope(k_rope)
    return (np.ascontiguousarray(q_nope), q_rope, np.ascontiguousarray(k_nope), k_rope, np.ascontiguousarray(v))


def e4m3fn_bytes(y):
    return np.clip(np.asarray(y, np.float64), -448.0, 448.0).astype(np.float32).astype(ml_dtypes.float8_e4m3fn).view(np.uint8)


def e4m3fn_values(b):
    return np.asarray(b, np.uint8).view(ml_dtypes.float8_e4m3fn).astype(np.float64)


def setup_inputs():
    d = draw0()
    x0 = np.asarray(d['w_up']).astype(np.float64)
    s = (np.max(np.abs(x0), axis=(1,), keepdims=True) / 448.0).astype(np.float32)
    out = {}
    for k, v in d.items():
        if k == 'w_up':
            out['w_up_bytes'] = e4m3fn_bytes(x0 / s.astype(np.float64))
            out['w_up_scale'] = s
        else:
            out[k] = v
    return out


def reference(x, w_down, rms_w, w_up_bytes, w_up_scale):
    return core(x, w_down, rms_w, e4m3fn_values(w_up_bytes) * w_up_scale.astype(np.float64))

@@ -1,0 +1,527 @@
+import math
+from contextlib import ExitStack
+
+import concourse.mybir as mybir
+from concourse.masks import make_identity
+
+S, D_MODEL, LAT, H, NOPE, ROPE = 512, 2048, 1536, 4, 256, 128
+D_HEAD = NOPE + ROPE
+THIRD = H * D_HEAD
+EPS = 1e-6
+FLOPS = 2 * S * (D_MODEL * LAT + LAT * 3 * THIRD)
+
+P = 128
+T = 4
+K_PASS = P * T
+G1 = D_MODEL // K_PASS
+G2 = LAT // K_PASS
+M_TILES = S // P
+BANK = 512
+HALF = 256
+PAIRS = 32
+
+F32 = mybir.dt.float32
+BF16 = mybir.dt.bfloat16
+I32 = mybir.dt.int32
+U32 = mybir.dt.uint32
+U8 = mybir.dt.uint8
+FP8 = mybir.dt.float8_e4m3fn
+FP8X4 = mybir.dt.float8_e4m3fn_x4
+ACT = mybir.ActivationFunctionType
+ALU = mybir.AluOpType
+
+
+STEPS_DOWN = 6
+STEPS_NORM = 7
+LAG = 2
+
+
+def lagged(jobs):
+    calls = []
+    for i in range(len(jobs) + LAG):
+        if i < len(jobs):
+            calls.append(jobs[i][0])
+        if i >= LAG:
+            calls.append(jobs[i - LAG][1])
+    return calls
+
+
+def tile_mhlattention_pa_kernel(
+    tc, x, w_down, rms_w, w_up_bytes, w_up_scale, out_0, out_1, out_2, out_3, out_4
+):
+    nc = tc.nc
+    with ExitStack() as ctx:
+        ctx.enter_context(tc.manual_schedule())
+        keep = ctx.enter_context(tc.tile_pool(name="keep", bufs=1))
+        pool = ctx.enter_context(tc.tile_pool(name="work", bufs=2))
+        psum = ctx.enter_context(tc.psum_pool(name="psum", bufs=2))
+
+        def acc_bank(name):
+            return psum.tile([P, BANK], F32, name=name, tag="acc", bufs=6)
+
+        up_raw = {}
+        down_raw = {}
+        x_raw = {}
+
+        def load_up(third, g):
+            t = pool.tile([P, T, THIRD], U8, name="up_raw", tag="up_raw", bufs=4, align_bytes=64)
+            rows = w_up_bytes[g * K_PASS : (g + 1) * K_PASS, third * THIRD : (third + 1) * THIRD]
+            nc.sync.dma_start(out=t[:], in_=rows.rearrange("(p t) n -> p t n", t=T))
+            up_raw[third, g] = t
+
+        def load_down(g):
+            t = pool.tile([P, T, LAT], BF16, name="down_raw", tag="down_raw", bufs=2, align_bytes=64)
+            rows = w_down[g * K_PASS : (g + 1) * K_PASS, :]
+            nc.sync.dma_start(out=t[:], in_=rows.rearrange("(p t) n -> p t n", t=T))
+            down_raw[g] = t
+
+        def load_x(m):
+            t = pool.tile([P, D_MODEL], BF16, name="x_raw", tag="x_raw", bufs=4, align_bytes=64)
+            nc.sync.dma_start(out=t[:], in_=x[0, m * P : (m + 1) * P, :])
+            x_raw[m] = t
+
+        warm = keep.tile([P, 1], F32, name="warm")
+        nc.gpsimd.memset(warm[:], 0.0)
+        nc.scalar.activation(out=warm[:], in_=warm[:], func=ACT.Sin)
+        ident_f = keep.tile([P, P], F32, name="ident_f", align_bytes=64)
+        make_identity(nc, ident_f[:])
+        ident_b = keep.tile([P, P], BF16, name="ident_b", align_bytes=64)
+        nc.vector.tensor_copy(out=ident_b[:], in_=ident_f[:])
+
+        scale = keep.tile([P, G2, T], F32, name="scale")
+        nc.sync.dma_start(out=scale[:], in_=w_up_scale.rearrange("(g p t) o -> p g (t o)", p=P, t=T))
+        load_up(0, 0)
+        for m in range(M_TILES):
+            load_x(m)
+        load_down(0)
+        load_up(0, 1)
+        load_down(1)
+        load_up(0, 2)
+
+        freq = keep.tile([P, PAIRS], F32, name="freq")
+        nc.vector.memset(freq[:, 0:1], 1.0)
+        n = 1
+        while n < PAIRS:
+            nc.vector.tensor_scalar(
+                out=freq[:, n : 2 * n], in0=freq[:, 0:n], scalar1=10000.0 ** (-n / PAIRS), scalar2=None, op0=ALU.mult
+            )
+            n *= 2
+        pos = keep.tile([P, M_TILES], F32, name="pos")
+        nc.gpsimd.iota(
+            pos[:], pattern=[[P, M_TILES]], base=0, channel_multiplier=1, allow_small_or_imprecise_dtypes=True
+        )
+        turns = keep.tile([P, 2, M_TILES, PAIRS], F32, name="turns")
+        nc.vector.scalar_tensor_tensor(
+            out=turns[:, 0],
+            in0=freq[:].unsqueeze(1).to_broadcast([P, M_TILES, PAIRS]),
+            scalar=1.0 / (2.0 * math.pi),
+            in1=pos[:].unsqueeze(2).to_broadcast([P, M_TILES, PAIRS]),
+            op0=ALU.mult,
+            op1=ALU.mult,
+        )
+        nc.vector.tensor_scalar(out=turns[:, 1], in0=turns[:, 0], scalar1=0.25, scalar2=None, op0=ALU.add)
+        whole_i = keep.tile([P, 2, M_TILES, PAIRS], I32, name="whole_i")
+        nc.vector.tensor_copy(out=whole_i[:], in_=turns[:])
+        whole_f = keep.tile([P, 2, M_TILES, PAIRS], F32, name="whole_f")
+        nc.vector.tensor_copy(out=whole_f[:], in_=whole_i[:])
+        frac = keep.tile([P, 2, M_TILES, PAIRS], F32, name="frac")
+        nc.vector.tensor_tensor(out=frac[:], in0=turns[:], in1=whole_f[:], op=ALU.subtract)
+        over = keep.tile([P, 2, M_TILES, PAIRS], F32, name="over")
+        nc.vector.tensor_scalar(out=over[:], in0=frac[:], scalar1=0.5, scalar2=None, op0=ALU.is_gt)
+        nc.vector.tensor_tensor(out=frac[:], in0=frac[:], in1=over[:], op=ALU.subtract)
+        cos = keep.tile([P, M_TILES, PAIRS], F32, name="cos")
+        nc.scalar.activation(out=cos[:], in_=frac[:, 1], func=ACT.Sin, scale=2.0 * math.pi)
+        sin = keep.tile([P, M_TILES, PAIRS, 2], F32, name="sin")
+        nc.scalar.activation(out=sin[:, :, :, 0], in_=frac[:, 0], func=ACT.Sin, scale=-2.0 * math.pi)
+        nc.scalar.activation(out=sin[:, :, :, 1], in_=frac[:, 0], func=ACT.Sin, scale=2.0 * math.pi)
+        minus_half = keep.tile([P, 1], F32, name="minus_half")
+        nc.gpsimd.memset(minus_half[:], -0.5)
+
+        up_wide = {}
+        up_grouped = {}
+        up_codes = {}
+
+        def codes_tile():
+            codes = pool.tile([P, THIRD], U32, name="codes", tag="codes", bufs=9, align_bytes=64)
+            scales = pool.tile([P, THIRD], U8, name="scales", tag="scales", bufs=9, align_bytes=64)
+            return codes, scales
+
+        def group_tile():
+            return pool.tile([P, T * BANK], BF16, name="grouped", tag="grouped", bufs=5, align_bytes=64)
+
+        def quantise(pair, cols, grouped):
+            codes, scales = pair
+            nc.vector.quantize_mx(out=codes[:, cols].bitcast(FP8X4), scales=scales[:, cols], in_=grouped)
+
+        def widen(unit, t, engine):
+            third, g, c0, width = unit
+            if unit not in up_wide:
+                up_wide[unit] = pool.tile([P, T, width], BF16, name="wide", tag="wide", bufs=2, align_bytes=64)
+            dst = up_wide[unit][:, t, :]
+            src = up_raw[third, g][:, t, c0 : c0 + width].bitcast(FP8)
+            s = scale[:, g, t : t + 1]
+            if engine == "vector":
+                nc.vector.tensor_scalar(out=dst, in0=src, scalar1=s, scalar2=None, op0=ALU.mult)
+            else:
+                nc.scalar.activation(out=dst, in_=src, func=ACT.Copy, scale=s)
+
+        def group_up(unit, j):
+            grouped = group_tile()
+            nc.vector.tensor_copy(
+                out=grouped[:].rearrange("p (c i t) -> p c t i", i=4, t=T),
+                in_=up_wide[unit][:, :, j : j + BANK].rearrange("p t (c i) -> p c t i", i=4),
+            )
+            up_grouped[unit, j] = grouped
+
+        def code_up(unit, j):
+            third, g, c0, width = unit
+            if (third, g) not in up_codes:
+                up_codes[third, g] = codes_tile()
+            quantise(up_codes[third, g], slice(c0 + j, c0 + j + BANK), up_grouped[unit, j][:])
+
+        x_codes = {}
+        x_grouped = {}
+
+        def turn_x(m, half):
+            words = x_raw[m][:].bitcast(F32)
+            if half == 0:
+                x_grouped[m] = group_tile()
+            bank = psum.tile([P, 2, 2, P], F32, name="xt", tag="acc", bufs=6)
+            for gg in range(2):
+                w0 = 256 * (2 * half + gg)
+                for u in range(2):
+                    nc.tensor.transpose(bank[:, gg, u, :], words[:, w0 + u : w0 + 256 : 2], ident_f[:])
+            dst = x_grouped[m][:, half * 1024 : (half + 1) * 1024].bitcast(F32)
+            dst = dst.rearrange("p (g r u) -> p g r u", g=2, u=2)
+            src = bank[:].rearrange("p g u r -> p g r u")
+            nc.vector.tensor_copy(out=dst, in_=src)
+
+        def code_x(m):
+            codes = keep.tile([P, G1 * P], U32, name="x_codes%d" % m, align_bytes=64)
+            scales = keep.tile([P, G1 * P], U8, name="x_scales%d" % m, align_bytes=64)
+            x_codes[m] = (codes, scales)
+            quantise(x_codes[m], slice(0, G1 * P), x_grouped[m][:])
+
+        down_codes = {}
+        down_grouped = {}
+
+        def group_down(g, c):
+            grouped = group_tile()
+            for b in range(2):
+                bank = psum.tile([P, 1024], BF16, name="dt", tag="tr", bufs=2)
+                for q in range(2):
+                    n0 = c * BANK + b * HALF + q * P
+                    nc.tensor.matmul(
+                        out=bank[:, q * BANK : (q + 1) * BANK].rearrange("p (n t) -> p n t", t=T),
+                        lhsT=ident_b[:],
+                        rhs=down_raw[g][:, :, n0 : n0 + P].rearrange("p t n -> p n t"),
+                        start=True,
+                        stop=True,
+                    )
+                nc.scalar.copy(out=grouped[:, b * 1024 : (b + 1) * 1024], in_=bank[:])
+            down_grouped[g, c] = grouped
+
+        def code_down(g, c):
+            if g not in down_codes:
+                down_codes[g] = codes_tile()
+            quantise(down_codes[g], slice(c * BANK, (c + 1) * BANK), down_grouped[g, c][:])
+
+        latent = {}
+
+        def latent_pass(m, g):
+            if g == 0:
+                latent[m] = [acc_bank("h%d" % c) for c in range(LAT // BANK)]
+            xc, xs = x_codes[m]
+            dc, ds = down_codes[g]
+            for c in range(LAT // BANK):
+                nc.tensor.matmul_mx(
+                    out=latent[m][c][:],
+                    lhsT=xc[:, g * P : (g + 1) * P].bitcast(FP8X4),
+                    lhsT_scale=xs[:, g * P : (g + 1) * P],
+                    rhs=dc[:, c * BANK : (c + 1) * BANK].bitcast(FP8X4),
+                    rhs_scale=ds[:, c * BANK : (c + 1) * BANK],
+                    start=(g == 0),
+                    stop=(g == G1 - 1),
+                )
+
+        gain = keep.tile([P, LAT], BF16, name="gain", align_bytes=64)
+        n_codes = {}
+        n_grouped = {}
+        n_banks = {}
+        normed = {}
+        rstds = {}
+
+        def sum_squares(m):
+            sums = pool.tile([P, 3], F32, name="sums", tag="sums", bufs=2)
+            for c in range(3):
+                junk = pool.tile([P, BANK], BF16, name="junk", tag="junk", bufs=3)
+                nc.scalar.activation(
+                    out=junk[:], in_=latent[m][c][:], func=ACT.Square, accum_out=sums[:, c : c + 1]
+                )
+            mean = pool.tile([P, 3], F32, name="mean", tag="mean", bufs=2)
+            nc.gpsimd.tensor_scalar(
+                out=mean[:, 0:1], in0=sums[:, 0:1], scalar1=1.0 / LAT, scalar2=EPS, op0=ALU.mult, op1=ALU.add
+            )
+            for c in (1, 2):
+                nc.gpsimd.tensor_scalar(
+                    out=mean[:, c : c + 1],
+                    in0=sums[:, c : c + 1],
+                    scalar1=1.0 / LAT,
+                    scalar2=mean[:, c - 1 : c],
+                    op0=ALU.mult,
+                    op1=ALU.add,
+                )
+            rstd = pool.tile([P, 1], F32, name="rstd", tag="rstd", bufs=2)
+            nc.gpsimd.tensor_tensor(out=rstd[:], in0=mean[:, 2:3], in1=minus_half[:], op=ALU.pow)
+            rstds[m] = rstd
+
+        def normalise(m):
+            nm = pool.tile([P, LAT], BF16, name="normed", tag="normed", bufs=2, align_bytes=64)
+            for c in range(3):
+                cols = slice(c * BANK, (c + 1) * BANK)
+                nc.vector.scalar_tensor_tensor(
+                    out=nm[:, cols], in0=latent[m][c][:], scalar=rstds[m][:], in1=gain[:, cols], op0=ALU.mult, op1=ALU.mult
+                )
+            normed[m] = nm
+
+        N_PARTS = ((0, 2), (2, 1))
+
+        def turn_n(m):
+            words = normed[m][:].bitcast(F32)
+            n_banks[m] = []
+            for g0, count in N_PARTS:
+                bank = psum.tile([P, 2, 2, P], F32, name="nt", tag="tr", bufs=2)
+                n_banks[m].append(bank)
+                for gg in range(count):
+                    w0 = 256 * (g0 + gg)
+                    for u in range(2):
+                        nc.tensor.transpose(bank[:, gg, u, :], words[:, w0 + u : w0 + 256 : 2], ident_f[:])
+
+        def group_n(m):
+            n_grouped[m] = group_tile()
+            for (g0, count), bank in zip(N_PARTS, n_banks[m]):
+                elems = slice(g0 * BANK, (g0 + count) * BANK)
+                nc.scalar.copy(
+                    out=n_grouped[m][:, elems].bitcast(F32).rearrange("p (g r u) -> p g r u", g=count, u=2),
+                    in_=bank[:, 0:count].rearrange("p g u r -> p g r u"),
+                )
+
+        def code_n(m):
+            codes = keep.tile([P, G2 * P], U32, name="n_codes%d" % m, align_bytes=64)
+            scales = keep.tile([P, G2 * P], U8, name="n_scales%d" % m, align_bytes=64)
+            n_codes[m] = (codes, scales)
+            for g0, count in N_PARTS:
+                quantise(
+                    n_codes[m], slice(g0 * P, (g0 + count) * P), n_grouped[m][:, g0 * BANK : (g0 + count) * BANK]
+                )
+
+        def project(m, pieces, name):
+            bank = acc_bank(name)
+            col = 0
+            for third, c0, width in pieces:
+                for g in range(G2):
+                    codes, scales = up_codes[third, g]
+                    a, s = n_codes[m]
+                    nc.tensor.matmul_mx(
+                        out=bank[:, col : col + width],
+                        lhsT=a[:, g * P : (g + 1) * P].bitcast(FP8X4),
+                        lhsT_scale=s[:, g * P : (g + 1) * P],
+                        rhs=codes[:, c0 : c0 + width].bitcast(FP8X4),
+                        rhs_scale=scales[:, c0 : c0 + width],
+                        start=(g == 0),
+                        stop=(g == G2 - 1),
+                    )
+                col += width
+            return bank
+
+        def tokens(out, m):
+            return out[0].rearrange("h s d -> s h d")[m * P : (m + 1) * P]
+
+        def heads(bank):
+            return bank[:].rearrange("p (d h) -> p h d", h=H)
+
+        def out_tile(name):
+            return pool.tile([P, 1024], F32, name=name, tag="out", bufs=4)
+
+        outs = {}
+        banks = {}
+
+        def nope_project(m, third, c):
+            banks["nope", third, m, c] = project(m, [(third, c * BANK, BANK)], "nope_ps")
+
+        def nope_store(m, third, c):
+            if c == 0:
+                outs[third, m] = out_tile("nope")[:].rearrange("p (h d) -> p h d", h=H)
+            o = outs[third, m]
+            nc.scalar.copy(out=o[:, :, c * P : (c + 1) * P], in_=heads(banks["nope", third, m, c]))
+            if c == 1:
+                nc.sync.dma_start(out=tokens(out_0 if third == 0 else out_2, m), in_=o)
+
+        def rot_project(m):
+            banks["rot", m] = project(m, [(0, 1024, HALF), (1, 1024, HALF)], "rot_ps")
+
+        def rot_products(m):
+            bank = banks["rot", m]
+            r = bank[:].rearrange("p (q i e h) -> p q i e h", q=2, e=2, h=H)
+            t1 = pool.tile([P, BANK], F32, name="t1", tag="t1", bufs=2)
+            t2 = pool.tile([P, BANK], F32, name="t2", tag="t2", bufs=2)
+            nc.vector.tensor_tensor(
+                out=t1[:].rearrange("p (q i f) -> p q i f", q=2, f=2 * H),
+                in0=bank[:].rearrange("p (q i f) -> p q i f", q=2, f=2 * H),
+                in1=cos[:, m].unsqueeze(1).unsqueeze(3).to_broadcast([P, 2, PAIRS, 2 * H]),
+                op=ALU.mult,
+            )
+            nc.vector.tensor_tensor(
+                out=t2[:].rearrange("p (q i e h) -> p q i e h", q=2, e=2, h=H),
+                in0=r[:, :, :, ::-1, :],
+                in1=sin[:, m].unsqueeze(1).unsqueeze(4).to_broadcast([P, 2, PAIRS, 2, H]),
+                op=ALU.mult,
+            )
+            outs["t", m] = (t1, t2)
+
+        def pass_project(m):
+            banks["pass", m] = project(m, [(0, 1280, HALF), (1, 1280, HALF)], "pass_ps")
+
+        def rope_store(m):
+            o = out_tile("rope")[:].rearrange("p (q h d) -> p q h d", q=2, h=H)
+            t1, t2 = outs["t", m]
+            nc.vector.tensor_tensor(
+                out=o[:, :, :, 0:64],
+                in0=t1[:].rearrange("p (q d h) -> p q h d", q=2, h=H),
+                in1=t2[:].rearrange("p (q d h) -> p q h d", q=2, h=H),
+                op=ALU.add,
+            )
+            bank = banks["pass", m]
+            nc.scalar.copy(out=o[:, :, :, 64:128], in_=bank[:].rearrange("p (q d h) -> p q h d", q=2, h=H))
+            nc.sync.dma_start(out=tokens(out_1, m), in_=o[:, 0])
+            nc.sync.dma_start(out=tokens(out_3, m), in_=o[:, 1])
+
+        def value_project(m, c):
+            banks["v", m, c] = project(m, [(2, c * BANK, BANK)], "v_ps")
+
+        def value_store(m, c, engine):
+            o = out_tile("value")[:, 0:BANK].rearrange("p (h d) -> p h d", h=H)
+            if engine == "scalar":
+                nc.scalar.copy(out=o, in_=heads(banks["v", m, c]))
+            else:
+                nc.vector.tensor_copy(out=o, in_=heads(banks["v", m, c]))
+            nc.sync.dma_start(out=tokens(out_4, m)[:, :, c * P : (c + 1) * P], in_=o)
+
+        units = [(third, g, 0, THIRD) for third in (0, 1) for g in range(G2)]
+        units += [(2, g, c, BANK) for c in range(0, THIRD, BANK) for g in range(G2)]
+
+        chunks = [(unit, j) for unit in units for j in range(0, unit[3], BANK)]
+        steps = []
+        for n, (unit, j) in enumerate(chunks):
+            ahead = units.index(unit) + 1
+            todo = []
+            if ahead < len(units):
+                if unit[3] == BANK or units[ahead][3] < unit[3]:
+                    todo = [(units[ahead], t) for t in range(T)] if j + BANK == unit[3] else []
+                else:
+                    todo = [[(units[ahead], 0)], [(units[ahead], 1)], [(units[ahead], 2), (units[ahead], 3)]][j // BANK]
+            steps.append((todo, chunks[n], chunks[n - 1] if n else None))
+
+        def up_step(n):
+            if n == len(steps):
+                code_up(*chunks[-1])
+                return
+            todo, now, before = steps[n]
+            for unit, t in todo:
+                if t < 3:
+                    widen(unit, t, "scalar")
+            group_up(*now)
+            for unit, t in todo:
+                if t == 3:
+                    widen(unit, t, "vector")
+            if before:
+                code_up(*before)
+
+        done = [0]
+
+        def weave(main, count):
+            given = 0
+            for i, call in enumerate(main):
+                call()
+                while given < count * (i + 1) // len(main):
+                    up_step(done[0])
+                    done[0] += 1
+                    given += 1
+
+        for t in range(T):
+            widen(units[0], t, "scalar")
+        for m in range(M_TILES):
+            for half in range(2):
+                turn_x(m, half)
+            if m:
+                code_x(m - 1)
+        code_x(3)
+
+        main = []
+        for g in range(G1):
+            for c in range(3):
+                main.append(lambda g=g, c=c: group_down(g, c))
+                if (g, c) == (0, 2):
+                    main.append(lambda: (load_down(2), load_up(1, 0)))
+                if (g, c) == (1, 2):
+                    main.append(lambda: (load_down(3), load_up(1, 1)))
+                if c:
+                    main.append(lambda g=g, c=c: code_down(g, c - 1))
+                elif g:
+                    main.append(lambda g=g: (code_down(g - 1, 2), latent_pass(0, g - 1), latent_pass(1, g - 1)))
+        main.append(lambda: (code_down(3, 2), latent_pass(0, 3), latent_pass(1, 3)))
+        weave(main, STEPS_DOWN)
+
+        nc.sync.dma_start(out=gain[:], in_=rms_w.partition_broadcast(P))
+        load_up(1, 2)
+        load_up(2, 0)
+        load_up(2, 1)
+        load_up(2, 2)
+        main = [
+            lambda: sum_squares(0),
+            lambda: sum_squares(1),
+            lambda: normalise(0),
+            lambda: turn_n(0),
+            lambda: [latent_pass(2, g) for g in range(G1)],
+            lambda: normalise(1),
+            lambda: turn_n(1) if False else None,
+            lambda: group_n(0),
+            lambda: turn_n(1),
+            lambda: [latent_pass(3, g) for g in range(G1)],
+            lambda: code_n(0),
+            lambda: group_n(1),
+            lambda: sum_squares(2),
+            lambda: code_n(1),
+            lambda: sum_squares(3),
+            lambda: normalise(2),
+            lambda: turn_n(2),
+            lambda: normalise(3),
+            lambda: group_n(2),
+            lambda: turn_n(3),
+            lambda: code_n(2),
+            lambda: group_n(3),
+            lambda: code_n(3),
+        ]
+        weave(main, STEPS_NORM)
+
+        jobs = [(lambda m=m, c=c: nope_project(m, 0, c), lambda m=m, c=c: nope_store(m, 0, c)) for m in range(M_TILES) for c in range(2)]
+        weave(lagged(jobs), 18 + 1 - done[0])
+        jobs = []
+        for m in range(M_TILES):
+            jobs.append((lambda m=m: rot_project(m), lambda m=m: rot_products(m)))
+            for c in range(2):
+                jobs.append((lambda m=m, c=c: nope_project(m, 1, c), lambda m=m, c=c: nope_store(m, 1, c)))
+            jobs.append((lambda m=m: pass_project(m), lambda m=m: rope_store(m)))
+        weave(lagged(jobs[:8]), 22 - done[0])
+        v0 = [(lambda m=m: value_project(m, 0), lambda m=m: value_store(m, 0, "scalar")) for m in range(M_TILES)]
+        rest = jobs[8:]
+        jobs = []
+        for i in range(4):
+            jobs += [rest[2 * i], v0[i], rest[2 * i + 1]]
+        weave(lagged(jobs), 25 - done[0])
+        jobs = [(lambda m=m: value_project(m, 1), lambda m=m: value_store(m, 1, "scalar")) for m in range(M_TILES)]
+        weave(lagged(jobs), 28 - done[0])
+        for m in range(M_TILES):
+            value_project(m, 2)
+        for m in range(M_TILES):
+            value_store(m, 2, "scalar" if m % 2 == 0 else "vector")

@@ -31,18 +31,23 @@ ACT = mybir.ActivationFunctionType
 ALU = mybir.AluOpType
 
 
-STEPS_DOWN = 6
-STEPS_NORM = 7
+STEPS_DOWN = 8
+K1 = 8
+K2 = 12
 LAG = 2
+DOWN_EVERY = 2
+V_FROM = 3
+V2_FROM = 99
+W0 = 3
 
 
-def lagged(jobs):
+def lagged(jobs, lag):
     calls = []
-    for i in range(len(jobs) + LAG):
+    for i in range(len(jobs) + lag):
         if i < len(jobs):
             calls.append(jobs[i][0])
-        if i >= LAG:
-            calls.append(jobs[i - LAG][1])
+        if i >= lag:
+            calls.append(jobs[i - lag][1])
     return calls
 
 
@@ -55,6 +60,8 @@ def tile_mhlattention_pa_kernel(
         keep = ctx.enter_context(tc.tile_pool(name="keep", bufs=1))
         pool = ctx.enter_context(tc.tile_pool(name="work", bufs=2))
         psum = ctx.enter_context(tc.psum_pool(name="psum", bufs=2))
+        early = []
+        late = []
 
         def acc_bank(name):
             return psum.tile([P, BANK], F32, name=name, tag="acc", bufs=6)
@@ -70,13 +77,13 @@ def tile_mhlattention_pa_kernel(
             up_raw[third, g] = t
 
         def load_down(g):
-            t = pool.tile([P, T, LAT], BF16, name="down_raw", tag="down_raw", bufs=2, align_bytes=64)
+            t = early[0].tile([P, T, LAT], BF16, name="down_raw", tag="down_raw", bufs=3, align_bytes=64)
             rows = w_down[g * K_PASS : (g + 1) * K_PASS, :]
             nc.sync.dma_start(out=t[:], in_=rows.rearrange("(p t) n -> p t n", t=T))
             down_raw[g] = t
 
         def load_x(m):
-            t = pool.tile([P, D_MODEL], BF16, name="x_raw", tag="x_raw", bufs=4, align_bytes=64)
+            t = early[0].tile([P, D_MODEL], BF16, name="x_raw", tag="x_raw", bufs=4, align_bytes=64)
             nc.sync.dma_start(out=t[:], in_=x[0, m * P : (m + 1) * P, :])
             x_raw[m] = t
 
@@ -85,18 +92,9 @@ def tile_mhlattention_pa_kernel(
         nc.scalar.activation(out=warm[:], in_=warm[:], func=ACT.Sin)
         ident_f = keep.tile([P, P], F32, name="ident_f", align_bytes=64)
         make_identity(nc, ident_f[:])
-        ident_b = keep.tile([P, P], BF16, name="ident_b", align_bytes=64)
-        nc.vector.tensor_copy(out=ident_b[:], in_=ident_f[:])
 
         scale = keep.tile([P, G2, T], F32, name="scale")
         nc.sync.dma_start(out=scale[:], in_=w_up_scale.rearrange("(g p t) o -> p g (t o)", p=P, t=T))
-        load_up(0, 0)
-        for m in range(M_TILES):
-            load_x(m)
-        load_down(0)
-        load_up(0, 1)
-        load_down(1)
-        load_up(0, 2)
 
         freq = keep.tile([P, PAIRS], F32, name="freq")
         nc.vector.memset(freq[:, 0:1], 1.0)
@@ -129,11 +127,6 @@ def tile_mhlattention_pa_kernel(
         over = keep.tile([P, 2, M_TILES, PAIRS], F32, name="over")
         nc.vector.tensor_scalar(out=over[:], in0=frac[:], scalar1=0.5, scalar2=None, op0=ALU.is_gt)
         nc.vector.tensor_tensor(out=frac[:], in0=frac[:], in1=over[:], op=ALU.subtract)
-        cos = keep.tile([P, M_TILES, PAIRS], F32, name="cos")
-        nc.scalar.activation(out=cos[:], in_=frac[:, 1], func=ACT.Sin, scale=2.0 * math.pi)
-        sin = keep.tile([P, M_TILES, PAIRS, 2], F32, name="sin")
-        nc.scalar.activation(out=sin[:, :, :, 0], in_=frac[:, 0], func=ACT.Sin, scale=-2.0 * math.pi)
-        nc.scalar.activation(out=sin[:, :, :, 1], in_=frac[:, 0], func=ACT.Sin, scale=2.0 * math.pi)
         minus_half = keep.tile([P, 1], F32, name="minus_half")
         nc.gpsimd.memset(minus_half[:], -0.5)
 
@@ -156,7 +149,7 @@ def tile_mhlattention_pa_kernel(
         def widen(unit, t, engine):
             third, g, c0, width = unit
             if unit not in up_wide:
-                up_wide[unit] = pool.tile([P, T, width], BF16, name="wide", tag="wide", bufs=2, align_bytes=64)
+                up_wide[unit] = pool.tile([P, T, width], BF16, name="wide", tag="wide%d" % width, bufs=2 if width > BANK else 3, align_bytes=64)
             dst = up_wide[unit][:, t, :]
             src = up_raw[third, g][:, t, c0 : c0 + width].bitcast(FP8)
             s = scale[:, g, t : t + 1]
@@ -197,8 +190,8 @@ def tile_mhlattention_pa_kernel(
             nc.vector.tensor_copy(out=dst, in_=src)
 
         def code_x(m):
-            codes = keep.tile([P, G1 * P], U32, name="x_codes%d" % m, align_bytes=64)
-            scales = keep.tile([P, G1 * P], U8, name="x_scales%d" % m, align_bytes=64)
+            codes = early[0].tile([P, G1 * P], U32, name="x_codes%d" % m, align_bytes=64)
+            scales = early[0].tile([P, G1 * P], U8, name="x_scales%d" % m, align_bytes=64)
             x_codes[m] = (codes, scales)
             quantise(x_codes[m], slice(0, G1 * P), x_grouped[m][:])
 
@@ -207,18 +200,12 @@ def tile_mhlattention_pa_kernel(
 
         def group_down(g, c):
             grouped = group_tile()
-            for b in range(2):
-                bank = psum.tile([P, 1024], BF16, name="dt", tag="tr", bufs=2)
-                for q in range(2):
-                    n0 = c * BANK + b * HALF + q * P
-                    nc.tensor.matmul(
-                        out=bank[:, q * BANK : (q + 1) * BANK].rearrange("p (n t) -> p n t", t=T),
-                        lhsT=ident_b[:],
-                        rhs=down_raw[g][:, :, n0 : n0 + P].rearrange("p t n -> p n t"),
-                        start=True,
-                        stop=True,
-                    )
-                nc.scalar.copy(out=grouped[:, b * 1024 : (b + 1) * 1024], in_=bank[:])
+            dst = grouped[:].rearrange("p (c i t) -> p c t i", i=4, t=T)
+            src = down_raw[g][:, :, c * BANK : (c + 1) * BANK].rearrange("p t (c i) -> p c t i", i=4)
+            if (3 * g + c) % DOWN_EVERY == 1:
+                nc.scalar.copy(out=dst, in_=src)
+            else:
+                nc.vector.tensor_copy(out=dst, in_=src)
             down_grouped[g, c] = grouped
 
         def code_down(g, c):
@@ -341,7 +328,7 @@ def tile_mhlattention_pa_kernel(
             return bank[:].rearrange("p (d h) -> p h d", h=H)
 
         def out_tile(name):
-            return pool.tile([P, 1024], F32, name=name, tag="out", bufs=4)
+            return late[0].tile([P, 1024], F32, name=name, tag="out", bufs=8)
 
         outs = {}
         banks = {}
@@ -363,8 +350,8 @@ def tile_mhlattention_pa_kernel(
         def rot_products(m):
             bank = banks["rot", m]
             r = bank[:].rearrange("p (q i e h) -> p q i e h", q=2, e=2, h=H)
-            t1 = pool.tile([P, BANK], F32, name="t1", tag="t1", bufs=2)
-            t2 = pool.tile([P, BANK], F32, name="t2", tag="t2", bufs=2)
+            t1 = late[0].tile([P, BANK], F32, name="t1", tag="t1", bufs=2)
+            t2 = late[0].tile([P, BANK], F32, name="t2", tag="t2", bufs=2)
             nc.vector.tensor_tensor(
                 out=t1[:].rearrange("p (q i f) -> p q i f", q=2, f=2 * H),
                 in0=bank[:].rearrange("p (q i f) -> p q i f", q=2, f=2 * H),
@@ -422,105 +409,144 @@ def tile_mhlattention_pa_kernel(
                     todo = [[(units[ahead], 0)], [(units[ahead], 1)], [(units[ahead], 2), (units[ahead], 3)]][j // BANK]
             steps.append((todo, chunks[n], chunks[n - 1] if n else None))
 
+        cos = keep.tile([P, M_TILES, PAIRS], F32, name="cos")
+        sin = keep.tile([P, M_TILES, PAIRS, 2], F32, name="sin")
+
+        def on_vector(unit, t):
+            return (t == 3 and units.index(unit) >= V_FROM) or (t == 2 and units.index(unit) >= V2_FROM)
+
+        def rope_tables():
+            nc.scalar.activation(out=cos[:], in_=frac[:, 1], func=ACT.Sin, scale=2.0 * math.pi)
+            nc.scalar.activation(out=sin[:, :, :, 0], in_=frac[:, 0], func=ACT.Sin, scale=-2.0 * math.pi)
+            nc.scalar.activation(out=sin[:, :, :, 1], in_=frac[:, 0], func=ACT.Sin, scale=2.0 * math.pi)
+
         def up_step(n):
             if n == len(steps):
                 code_up(*chunks[-1])
                 return
             todo, now, before = steps[n]
             for unit, t in todo:
-                if t < 3:
+                if not on_vector(unit, t):
                     widen(unit, t, "scalar")
             group_up(*now)
             for unit, t in todo:
-                if t == 3:
+                if on_vector(unit, t):
                     widen(unit, t, "vector")
             if before:
                 code_up(*before)
 
         done = [0]
 
-        def weave(main, count):
-            given = 0
-            for i, call in enumerate(main):
+        def up():
+            up_step(done[0])
+            done[0] += 1
+
+        def run(calls):
+            for call in calls:
                 call()
-                while given < count * (i + 1) // len(main):
-                    up_step(done[0])
-                    done[0] += 1
+
+        def spread(calls, count):
+            given = 0
+            for i, call in enumerate(calls):
+                call()
+                while given < count * (i + 1) // len(calls):
+                    up()
                     given += 1
 
-        for t in range(T):
-            widen(units[0], t, "scalar")
-        for m in range(M_TILES):
-            for half in range(2):
-                turn_x(m, half)
-            if m:
-                code_x(m - 1)
-        code_x(3)
+        with tc.tile_pool(name="early", bufs=1) as early_pool:
+            early.append(early_pool)
+            load_up(0, 0)
+            for m in range(M_TILES):
+                load_x(m)
+            load_down(0)
+            load_up(0, 1)
+            load_down(1)
+            load_up(0, 2)
+            for t in range(T):
+                widen(units[0], t, "scalar" if t < W0 else "vector")
+            for m in range(M_TILES):
+                for half in range(2):
+                    turn_x(m, half)
+                if m:
+                    code_x(m - 1)
+            rope_tables()
+            code_x(3)
 
-        main = []
-        for g in range(G1):
-            for c in range(3):
-                main.append(lambda g=g, c=c: group_down(g, c))
-                if (g, c) == (0, 2):
-                    main.append(lambda: (load_down(2), load_up(1, 0)))
-                if (g, c) == (1, 2):
-                    main.append(lambda: (load_down(3), load_up(1, 1)))
-                if c:
-                    main.append(lambda g=g, c=c: code_down(g, c - 1))
-                elif g:
-                    main.append(lambda g=g: (code_down(g - 1, 2), latent_pass(0, g - 1), latent_pass(1, g - 1)))
-        main.append(lambda: (code_down(3, 2), latent_pass(0, 3), latent_pass(1, 3)))
-        weave(main, STEPS_DOWN)
+            calls = []
+            for i in range(13):
+                if i < 12:
+                    calls.append(lambda i=i: group_down(*divmod(i, 3)))
+                if i == 1:
+                    calls.append(lambda: (load_down(2), load_up(1, 0)))
+                if i == 4:
+                    calls.append(lambda: (load_down(3), load_up(1, 1)))
+                if i:
+                    calls.append(lambda i=i: code_down(*divmod(i - 1, 3)))
+                    if i % 3 == 0:
+                        calls.append(lambda i=i: (latent_pass(0, i // 3 - 1), latent_pass(1, i // 3 - 1)))
+            spread(calls, STEPS_DOWN)
 
-        nc.sync.dma_start(out=gain[:], in_=rms_w.partition_broadcast(P))
-        load_up(1, 2)
-        load_up(2, 0)
-        load_up(2, 1)
-        load_up(2, 2)
-        main = [
-            lambda: sum_squares(0),
-            lambda: sum_squares(1),
-            lambda: normalise(0),
-            lambda: turn_n(0),
-            lambda: [latent_pass(2, g) for g in range(G1)],
-            lambda: normalise(1),
-            lambda: turn_n(1) if False else None,
-            lambda: group_n(0),
-            lambda: turn_n(1),
-            lambda: [latent_pass(3, g) for g in range(G1)],
-            lambda: code_n(0),
-            lambda: group_n(1),
-            lambda: sum_squares(2),
-            lambda: code_n(1),
-            lambda: sum_squares(3),
-            lambda: normalise(2),
-            lambda: turn_n(2),
-            lambda: normalise(3),
-            lambda: group_n(2),
-            lambda: turn_n(3),
-            lambda: code_n(2),
+            nc.sync.dma_start(out=gain[:], in_=rms_w.partition_broadcast(P))
+            load_up(1, 2)
+            load_up(2, 0)
+            load_up(2, 1)
+            load_up(2, 2)
+            run([
+                lambda: sum_squares(0),
+                lambda: sum_squares(1),
+                up,
+                lambda: normalise(0),
+                lambda: turn_n(0),
+                lambda: [latent_pass(2, g) for g in range(G1)],
+                lambda: normalise(1),
+                up,
+                lambda: group_n(0),
+                lambda: turn_n(1),
+                lambda: [latent_pass(3, g) for g in range(G1)],
+                lambda: code_n(0),
+                up,
+                lambda: sum_squares(2),
+                lambda: group_n(1),
+                lambda: code_n(1),
+                up,
+                lambda: normalise(2),
+                lambda: turn_n(2),
+                lambda: sum_squares(3),
+                up,
+                lambda: group_n(2),
+                lambda: code_n(2),
+                lambda: normalise(3),
+                lambda: turn_n(3),
+            ])
+        late.append(ctx.enter_context(tc.tile_pool(name="late", bufs=2)))
+        run([
+            lambda: nope_project(0, 0, 0),
+            lambda: nope_project(0, 0, 1),
+            lambda: nope_project(1, 0, 0),
+            up,
             lambda: group_n(3),
             lambda: code_n(3),
+        ])
+        jobs = [
+            (lambda m=m, c=c: nope_project(m, 0, c), lambda m=m, c=c: nope_store(m, 0, c))
+            for m in range(M_TILES)
+            for c in range(2)
         ]
-        weave(main, STEPS_NORM)
-
-        jobs = [(lambda m=m, c=c: nope_project(m, 0, c), lambda m=m, c=c: nope_store(m, 0, c)) for m in range(M_TILES) for c in range(2)]
-        weave(lagged(jobs), 18 + 1 - done[0])
-        jobs = []
+        order = lagged(jobs, 3)[3:]
+        spread(order, 19 - done[0])
+        kjobs = []
         for m in range(M_TILES):
-            jobs.append((lambda m=m: rot_project(m), lambda m=m: rot_products(m)))
+            kjobs.append((lambda m=m: rot_project(m), lambda m=m: rot_products(m)))
             for c in range(2):
-                jobs.append((lambda m=m, c=c: nope_project(m, 1, c), lambda m=m, c=c: nope_store(m, 1, c)))
-            jobs.append((lambda m=m: pass_project(m), lambda m=m: rope_store(m)))
-        weave(lagged(jobs[:8]), 22 - done[0])
-        v0 = [(lambda m=m: value_project(m, 0), lambda m=m: value_store(m, 0, "scalar")) for m in range(M_TILES)]
-        rest = jobs[8:]
-        jobs = []
-        for i in range(4):
-            jobs += [rest[2 * i], v0[i], rest[2 * i + 1]]
-        weave(lagged(jobs), 25 - done[0])
-        jobs = [(lambda m=m: value_project(m, 1), lambda m=m: value_store(m, 1, "scalar")) for m in range(M_TILES)]
-        weave(lagged(jobs), 28 - done[0])
+                kjobs.append((lambda m=m, c=c: nope_project(m, 1, c), lambda m=m, c=c: nope_store(m, 1, c)))
+            kjobs.append((lambda m=m: pass_project(m), lambda m=m: rope_store(m)))
+        vjobs = [
+            [(lambda m=m, c=c: value_project(m, c), lambda m=m, c=c: value_store(m, c, "scalar")) for m in range(M_TILES)]
+            for c in range(2)
+        ]
+        spread(lagged(kjobs[:K1], LAG), 22 - done[0])
+        spread(lagged(kjobs[K1:K2] + vjobs[0], LAG), 25 - done[0])
+        spread(lagged(kjobs[K2:] + vjobs[1], LAG), 28 - done[0])
         for m in range(M_TILES):
             value_project(m, 2)
         for m in range(M_TILES):

import math
from contextlib import ExitStack

import concourse.mybir as mybir
from concourse.masks import make_identity

S, D_MODEL, LAT, H, NOPE, ROPE = 512, 2048, 1536, 4, 256, 128
D_HEAD = NOPE + ROPE
THIRD = H * D_HEAD
EPS = 1e-6
FLOPS = 2 * S * (D_MODEL * LAT + LAT * 3 * THIRD)

P = 128
T = 4
K_PASS = P * T
G1 = D_MODEL // K_PASS
G2 = LAT // K_PASS
M_TILES = S // P
BANK = 512
HALF = 256
PAIRS = 32

F32 = mybir.dt.float32
BF16 = mybir.dt.bfloat16
I32 = mybir.dt.int32
U32 = mybir.dt.uint32
U8 = mybir.dt.uint8
FP8 = mybir.dt.float8_e4m3fn
FP8X4 = mybir.dt.float8_e4m3fn_x4
ACT = mybir.ActivationFunctionType
ALU = mybir.AluOpType


STEPS_DOWN = 8
K1 = 8
K2 = 12
LAG = 2
DOWN_EVERY = 2
V_FROM = 3
V2_FROM = 99
W0 = 3


def lagged(jobs, lag):
    calls = []
    for i in range(len(jobs) + lag):
        if i < len(jobs):
            calls.append(jobs[i][0])
        if i >= lag:
            calls.append(jobs[i - lag][1])
    return calls


def tile_mhlattention_pa_kernel(
    tc, x, w_down, rms_w, w_up_bytes, w_up_scale, out_0, out_1, out_2, out_3, out_4
):
    nc = tc.nc
    with ExitStack() as ctx:
        ctx.enter_context(tc.manual_schedule())
        keep = ctx.enter_context(tc.tile_pool(name="keep", bufs=1))
        pool = ctx.enter_context(tc.tile_pool(name="work", bufs=2))
        psum = ctx.enter_context(tc.psum_pool(name="psum", bufs=2))
        early = []
        late = []

        def acc_bank(name):
            return psum.tile([P, BANK], F32, name=name, tag="acc", bufs=6)

        up_raw = {}
        down_raw = {}
        x_raw = {}

        def load_up(third, g):
            t = pool.tile([P, T, THIRD], U8, name="up_raw", tag="up_raw", bufs=4, align_bytes=64)
            rows = w_up_bytes[g * K_PASS : (g + 1) * K_PASS, third * THIRD : (third + 1) * THIRD]
            nc.sync.dma_start(out=t[:], in_=rows.rearrange("(p t) n -> p t n", t=T))
            up_raw[third, g] = t

        def load_down(g):
            t = early[0].tile([P, T, LAT], BF16, name="down_raw", tag="down_raw", bufs=3, align_bytes=64)
            rows = w_down[g * K_PASS : (g + 1) * K_PASS, :]
            nc.sync.dma_start(out=t[:], in_=rows.rearrange("(p t) n -> p t n", t=T))
            down_raw[g] = t

        def load_x(m):
            t = early[0].tile([P, D_MODEL], BF16, name="x_raw", tag="x_raw", bufs=4, align_bytes=64)
            nc.sync.dma_start(out=t[:], in_=x[0, m * P : (m + 1) * P, :])
            x_raw[m] = t

        warm = keep.tile([P, 1], F32, name="warm")
        nc.gpsimd.memset(warm[:], 0.0)
        nc.scalar.activation(out=warm[:], in_=warm[:], func=ACT.Sin)
        ident_f = keep.tile([P, P], F32, name="ident_f", align_bytes=64)
        make_identity(nc, ident_f[:])

        scale = keep.tile([P, G2, T], F32, name="scale")
        nc.sync.dma_start(out=scale[:], in_=w_up_scale.rearrange("(g p t) o -> p g (t o)", p=P, t=T))

        freq = keep.tile([P, PAIRS], F32, name="freq")
        nc.vector.memset(freq[:, 0:1], 1.0)
        n = 1
        while n < PAIRS:
            nc.vector.tensor_scalar(
                out=freq[:, n : 2 * n], in0=freq[:, 0:n], scalar1=10000.0 ** (-n / PAIRS), scalar2=None, op0=ALU.mult
            )
            n *= 2
        pos = keep.tile([P, M_TILES], F32, name="pos")
        nc.gpsimd.iota(
            pos[:], pattern=[[P, M_TILES]], base=0, channel_multiplier=1, allow_small_or_imprecise_dtypes=True
        )
        turns = keep.tile([P, 2, M_TILES, PAIRS], F32, name="turns")
        nc.vector.scalar_tensor_tensor(
            out=turns[:, 0],
            in0=freq[:].unsqueeze(1).to_broadcast([P, M_TILES, PAIRS]),
            scalar=1.0 / (2.0 * math.pi),
            in1=pos[:].unsqueeze(2).to_broadcast([P, M_TILES, PAIRS]),
            op0=ALU.mult,
            op1=ALU.mult,
        )
        nc.vector.tensor_scalar(out=turns[:, 1], in0=turns[:, 0], scalar1=0.25, scalar2=None, op0=ALU.add)
        whole_i = keep.tile([P, 2, M_TILES, PAIRS], I32, name="whole_i")
        nc.vector.tensor_copy(out=whole_i[:], in_=turns[:])
        whole_f = keep.tile([P, 2, M_TILES, PAIRS], F32, name="whole_f")
        nc.vector.tensor_copy(out=whole_f[:], in_=whole_i[:])
        frac = keep.tile([P, 2, M_TILES, PAIRS], F32, name="frac")
        nc.vector.tensor_tensor(out=frac[:], in0=turns[:], in1=whole_f[:], op=ALU.subtract)
        over = keep.tile([P, 2, M_TILES, PAIRS], F32, name="over")
        nc.vector.tensor_scalar(out=over[:], in0=frac[:], scalar1=0.5, scalar2=None, op0=ALU.is_gt)
        nc.vector.tensor_tensor(out=frac[:], in0=frac[:], in1=over[:], op=ALU.subtract)
        minus_half = keep.tile([P, 1], F32, name="minus_half")
        nc.gpsimd.memset(minus_half[:], -0.5)

        up_wide = {}
        up_grouped = {}
        up_codes = {}

        def codes_tile():
            codes = pool.tile([P, THIRD], U32, name="codes", tag="codes", bufs=9, align_bytes=64)
            scales = pool.tile([P, THIRD], U8, name="scales", tag="scales", bufs=9, align_bytes=64)
            return codes, scales

        def group_tile():
            return pool.tile([P, T * BANK], BF16, name="grouped", tag="grouped", bufs=5, align_bytes=64)

        def quantise(pair, cols, grouped):
            codes, scales = pair
            nc.vector.quantize_mx(out=codes[:, cols].bitcast(FP8X4), scales=scales[:, cols], in_=grouped)

        def widen(unit, t, engine):
            third, g, c0, width = unit
            if unit not in up_wide:
                up_wide[unit] = pool.tile([P, T, width], BF16, name="wide", tag="wide%d" % width, bufs=2 if width > BANK else 3, align_bytes=64)
            dst = up_wide[unit][:, t, :]
            src = up_raw[third, g][:, t, c0 : c0 + width].bitcast(FP8)
            s = scale[:, g, t : t + 1]
            if engine == "vector":
                nc.vector.tensor_scalar(out=dst, in0=src, scalar1=s, scalar2=None, op0=ALU.mult)
            else:
                nc.scalar.activation(out=dst, in_=src, func=ACT.Copy, scale=s)

        def group_up(unit, j):
            grouped = group_tile()
            nc.vector.tensor_copy(
                out=grouped[:].rearrange("p (c i t) -> p c t i", i=4, t=T),
                in_=up_wide[unit][:, :, j : j + BANK].rearrange("p t (c i) -> p c t i", i=4),
            )
            up_grouped[unit, j] = grouped

        def code_up(unit, j):
            third, g, c0, width = unit
            if (third, g) not in up_codes:
                up_codes[third, g] = codes_tile()
            quantise(up_codes[third, g], slice(c0 + j, c0 + j + BANK), up_grouped[unit, j][:])

        x_codes = {}
        x_grouped = {}

        def turn_x(m, half):
            words = x_raw[m][:].bitcast(F32)
            if half == 0:
                x_grouped[m] = group_tile()
            bank = psum.tile([P, 2, 2, P], F32, name="xt", tag="acc", bufs=6)
            for gg in range(2):
                w0 = 256 * (2 * half + gg)
                for u in range(2):
                    nc.tensor.transpose(bank[:, gg, u, :], words[:, w0 + u : w0 + 256 : 2], ident_f[:])
            dst = x_grouped[m][:, half * 1024 : (half + 1) * 1024].bitcast(F32)
            dst = dst.rearrange("p (g r u) -> p g r u", g=2, u=2)
            src = bank[:].rearrange("p g u r -> p g r u")
            nc.vector.tensor_copy(out=dst, in_=src)

        def code_x(m):
            codes = early[0].tile([P, G1 * P], U32, name="x_codes%d" % m, align_bytes=64)
            scales = early[0].tile([P, G1 * P], U8, name="x_scales%d" % m, align_bytes=64)
            x_codes[m] = (codes, scales)
            quantise(x_codes[m], slice(0, G1 * P), x_grouped[m][:])

        down_codes = {}
        down_grouped = {}

        def group_down(g, c):
            grouped = group_tile()
            dst = grouped[:].rearrange("p (c i t) -> p c t i", i=4, t=T)
            src = down_raw[g][:, :, c * BANK : (c + 1) * BANK].rearrange("p t (c i) -> p c t i", i=4)
            if (3 * g + c) % DOWN_EVERY == 1:
                nc.scalar.copy(out=dst, in_=src)
            else:
                nc.vector.tensor_copy(out=dst, in_=src)
            down_grouped[g, c] = grouped

        def code_down(g, c):
            if g not in down_codes:
                down_codes[g] = codes_tile()
            quantise(down_codes[g], slice(c * BANK, (c + 1) * BANK), down_grouped[g, c][:])

        latent = {}

        def latent_pass(m, g):
            if g == 0:
                latent[m] = [acc_bank("h%d" % c) for c in range(LAT // BANK)]
            xc, xs = x_codes[m]
            dc, ds = down_codes[g]
            for c in range(LAT // BANK):
                nc.tensor.matmul_mx(
                    out=latent[m][c][:],
                    lhsT=xc[:, g * P : (g + 1) * P].bitcast(FP8X4),
                    lhsT_scale=xs[:, g * P : (g + 1) * P],
                    rhs=dc[:, c * BANK : (c + 1) * BANK].bitcast(FP8X4),
                    rhs_scale=ds[:, c * BANK : (c + 1) * BANK],
                    start=(g == 0),
                    stop=(g == G1 - 1),
                )

        gain = keep.tile([P, LAT], BF16, name="gain", align_bytes=64)
        n_codes = {}
        n_grouped = {}
        n_banks = {}
        normed = {}
        rstds = {}

        def sum_squares(m):
            sums = pool.tile([P, 3], F32, name="sums", tag="sums", bufs=2)
            for c in range(3):
                junk = pool.tile([P, BANK], BF16, name="junk", tag="junk", bufs=3)
                nc.scalar.activation(
                    out=junk[:], in_=latent[m][c][:], func=ACT.Square, accum_out=sums[:, c : c + 1]
                )
            mean = pool.tile([P, 3], F32, name="mean", tag="mean", bufs=2)
            nc.gpsimd.tensor_scalar(
                out=mean[:, 0:1], in0=sums[:, 0:1], scalar1=1.0 / LAT, scalar2=EPS, op0=ALU.mult, op1=ALU.add
            )
            for c in (1, 2):
                nc.gpsimd.tensor_scalar(
                    out=mean[:, c : c + 1],
                    in0=sums[:, c : c + 1],
                    scalar1=1.0 / LAT,
                    scalar2=mean[:, c - 1 : c],
                    op0=ALU.mult,
                    op1=ALU.add,
                )
            rstd = pool.tile([P, 1], F32, name="rstd", tag="rstd", bufs=2)
            nc.gpsimd.tensor_tensor(out=rstd[:], in0=mean[:, 2:3], in1=minus_half[:], op=ALU.pow)
            rstds[m] = rstd

        def normalise(m):
            nm = pool.tile([P, LAT], BF16, name="normed", tag="normed", bufs=2, align_bytes=64)
            for c in range(3):
                cols = slice(c * BANK, (c + 1) * BANK)
                nc.vector.scalar_tensor_tensor(
                    out=nm[:, cols], in0=latent[m][c][:], scalar=rstds[m][:], in1=gain[:, cols], op0=ALU.mult, op1=ALU.mult
                )
            normed[m] = nm

        N_PARTS = ((0, 2), (2, 1))

        def turn_n(m):
            words = normed[m][:].bitcast(F32)
            n_banks[m] = []
            for g0, count in N_PARTS:
                bank = psum.tile([P, 2, 2, P], F32, name="nt", tag="tr", bufs=2)
                n_banks[m].append(bank)
                for gg in range(count):
                    w0 = 256 * (g0 + gg)
                    for u in range(2):
                        nc.tensor.transpose(bank[:, gg, u, :], words[:, w0 + u : w0 + 256 : 2], ident_f[:])

        def group_n(m):
            n_grouped[m] = group_tile()
            for (g0, count), bank in zip(N_PARTS, n_banks[m]):
                elems = slice(g0 * BANK, (g0 + count) * BANK)
                nc.scalar.copy(
                    out=n_grouped[m][:, elems].bitcast(F32).rearrange("p (g r u) -> p g r u", g=count, u=2),
                    in_=bank[:, 0:count].rearrange("p g u r -> p g r u"),
                )

        def code_n(m):
            codes = keep.tile([P, G2 * P], U32, name="n_codes%d" % m, align_bytes=64)
            scales = keep.tile([P, G2 * P], U8, name="n_scales%d" % m, align_bytes=64)
            n_codes[m] = (codes, scales)
            for g0, count in N_PARTS:
                quantise(
                    n_codes[m], slice(g0 * P, (g0 + count) * P), n_grouped[m][:, g0 * BANK : (g0 + count) * BANK]
                )

        def project(m, pieces, name):
            bank = acc_bank(name)
            col = 0
            for third, c0, width in pieces:
                for g in range(G2):
                    codes, scales = up_codes[third, g]
                    a, s = n_codes[m]
                    nc.tensor.matmul_mx(
                        out=bank[:, col : col + width],
                        lhsT=a[:, g * P : (g + 1) * P].bitcast(FP8X4),
                        lhsT_scale=s[:, g * P : (g + 1) * P],
                        rhs=codes[:, c0 : c0 + width].bitcast(FP8X4),
                        rhs_scale=scales[:, c0 : c0 + width],
                        start=(g == 0),
                        stop=(g == G2 - 1),
                    )
                col += width
            return bank

        def tokens(out, m):
            return out[0].rearrange("h s d -> s h d")[m * P : (m + 1) * P]

        def heads(bank):
            return bank[:].rearrange("p (d h) -> p h d", h=H)

        def out_tile(name):
            return late[0].tile([P, 1024], F32, name=name, tag="out", bufs=8)

        outs = {}
        banks = {}

        def nope_project(m, third, c):
            banks["nope", third, m, c] = project(m, [(third, c * BANK, BANK)], "nope_ps")

        def nope_store(m, third, c):
            if c == 0:
                outs[third, m] = out_tile("nope")[:].rearrange("p (h d) -> p h d", h=H)
            o = outs[third, m]
            nc.scalar.copy(out=o[:, :, c * P : (c + 1) * P], in_=heads(banks["nope", third, m, c]))
            if c == 1:
                nc.sync.dma_start(out=tokens(out_0 if third == 0 else out_2, m), in_=o)

        def rot_project(m):
            banks["rot", m] = project(m, [(0, 1024, HALF), (1, 1024, HALF)], "rot_ps")

        def rot_products(m):
            bank = banks["rot", m]
            r = bank[:].rearrange("p (q i e h) -> p q i e h", q=2, e=2, h=H)
            t1 = late[0].tile([P, BANK], F32, name="t1", tag="t1", bufs=2)
            t2 = late[0].tile([P, BANK], F32, name="t2", tag="t2", bufs=2)
            nc.vector.tensor_tensor(
                out=t1[:].rearrange("p (q i f) -> p q i f", q=2, f=2 * H),
                in0=bank[:].rearrange("p (q i f) -> p q i f", q=2, f=2 * H),
                in1=cos[:, m].unsqueeze(1).unsqueeze(3).to_broadcast([P, 2, PAIRS, 2 * H]),
                op=ALU.mult,
            )
            nc.vector.tensor_tensor(
                out=t2[:].rearrange("p (q i e h) -> p q i e h", q=2, e=2, h=H),
                in0=r[:, :, :, ::-1, :],
                in1=sin[:, m].unsqueeze(1).unsqueeze(4).to_broadcast([P, 2, PAIRS, 2, H]),
                op=ALU.mult,
            )
            outs["t", m] = (t1, t2)

        def pass_project(m):
            banks["pass", m] = project(m, [(0, 1280, HALF), (1, 1280, HALF)], "pass_ps")

        def rope_store(m):
            o = out_tile("rope")[:].rearrange("p (q h d) -> p q h d", q=2, h=H)
            t1, t2 = outs["t", m]
            nc.vector.tensor_tensor(
                out=o[:, :, :, 0:64],
                in0=t1[:].rearrange("p (q d h) -> p q h d", q=2, h=H),
                in1=t2[:].rearrange("p (q d h) -> p q h d", q=2, h=H),
                op=ALU.add,
            )
            bank = banks["pass", m]
            nc.scalar.copy(out=o[:, :, :, 64:128], in_=bank[:].rearrange("p (q d h) -> p q h d", q=2, h=H))
            nc.sync.dma_start(out=tokens(out_1, m), in_=o[:, 0])
            nc.sync.dma_start(out=tokens(out_3, m), in_=o[:, 1])

        def value_project(m, c):
            banks["v", m, c] = project(m, [(2, c * BANK, BANK)], "v_ps")

        def value_store(m, c, engine):
            o = out_tile("value")[:, 0:BANK].rearrange("p (h d) -> p h d", h=H)
            if engine == "scalar":
                nc.scalar.copy(out=o, in_=heads(banks["v", m, c]))
            else:
                nc.vector.tensor_copy(out=o, in_=heads(banks["v", m, c]))
            nc.sync.dma_start(out=tokens(out_4, m)[:, :, c * P : (c + 1) * P], in_=o)

        units = [(third, g, 0, THIRD) for third in (0, 1) for g in range(G2)]
        units += [(2, g, c, BANK) for c in range(0, THIRD, BANK) for g in range(G2)]

        chunks = [(unit, j) for unit in units for j in range(0, unit[3], BANK)]
        steps = []
        for n, (unit, j) in enumerate(chunks):
            ahead = units.index(unit) + 1
            todo = []
            if ahead < len(units):
                if unit[3] == BANK or units[ahead][3] < unit[3]:
                    todo = [(units[ahead], t) for t in range(T)] if j + BANK == unit[3] else []
                else:
                    todo = [[(units[ahead], 0)], [(units[ahead], 1)], [(units[ahead], 2), (units[ahead], 3)]][j // BANK]
            steps.append((todo, chunks[n], chunks[n - 1] if n else None))

        cos = keep.tile([P, M_TILES, PAIRS], F32, name="cos")
        sin = keep.tile([P, M_TILES, PAIRS, 2], F32, name="sin")

        def on_vector(unit, t):
            return (t == 3 and units.index(unit) >= V_FROM) or (t == 2 and units.index(unit) >= V2_FROM)

        def rope_tables():
            nc.scalar.activation(out=cos[:], in_=frac[:, 1], func=ACT.Sin, scale=2.0 * math.pi)
            nc.scalar.activation(out=sin[:, :, :, 0], in_=frac[:, 0], func=ACT.Sin, scale=-2.0 * math.pi)
            nc.scalar.activation(out=sin[:, :, :, 1], in_=frac[:, 0], func=ACT.Sin, scale=2.0 * math.pi)

        def up_step(n):
            if n == len(steps):
                code_up(*chunks[-1])
                return
            todo, now, before = steps[n]
            for unit, t in todo:
                if not on_vector(unit, t):
                    widen(unit, t, "scalar")
            group_up(*now)
            for unit, t in todo:
                if on_vector(unit, t):
                    widen(unit, t, "vector")
            if before:
                code_up(*before)

        done = [0]

        def up():
            up_step(done[0])
            done[0] += 1

        def run(calls):
            for call in calls:
                call()

        def spread(calls, count):
            given = 0
            for i, call in enumerate(calls):
                call()
                while given < count * (i + 1) // len(calls):
                    up()
                    given += 1

        with tc.tile_pool(name="early", bufs=1) as early_pool:
            early.append(early_pool)
            load_up(0, 0)
            for m in range(M_TILES):
                load_x(m)
            load_down(0)
            load_up(0, 1)
            load_down(1)
            load_up(0, 2)
            for t in range(T):
                widen(units[0], t, "scalar" if t < W0 else "vector")
            for m in range(M_TILES):
                for half in range(2):
                    turn_x(m, half)
                if m:
                    code_x(m - 1)
            rope_tables()
            code_x(3)

            calls = []
            for i in range(13):
                if i < 12:
                    calls.append(lambda i=i: group_down(*divmod(i, 3)))
                if i == 1:
                    calls.append(lambda: (load_down(2), load_up(1, 0)))
                if i == 4:
                    calls.append(lambda: (load_down(3), load_up(1, 1)))
                if i:
                    calls.append(lambda i=i: code_down(*divmod(i - 1, 3)))
                    if i % 3 == 0:
                        calls.append(lambda i=i: (latent_pass(0, i // 3 - 1), latent_pass(1, i // 3 - 1)))
            spread(calls, STEPS_DOWN)

            nc.sync.dma_start(out=gain[:], in_=rms_w.partition_broadcast(P))
            load_up(1, 2)
            load_up(2, 0)
            load_up(2, 1)
            load_up(2, 2)
            run([
                lambda: sum_squares(0),
                lambda: sum_squares(1),
                up,
                lambda: normalise(0),
                lambda: turn_n(0),
                lambda: [latent_pass(2, g) for g in range(G1)],
                lambda: normalise(1),
                up,
                lambda: group_n(0),
                lambda: turn_n(1),
                lambda: [latent_pass(3, g) for g in range(G1)],
                lambda: code_n(0),
                up,
                lambda: sum_squares(2),
                lambda: group_n(1),
                lambda: code_n(1),
                up,
                lambda: normalise(2),
                lambda: turn_n(2),
                lambda: sum_squares(3),
                up,
                lambda: group_n(2),
                lambda: code_n(2),
                lambda: normalise(3),
                lambda: turn_n(3),
            ])
        late.append(ctx.enter_context(tc.tile_pool(name="late", bufs=2)))
        run([
            lambda: nope_project(0, 0, 0),
            lambda: nope_project(0, 0, 1),
            lambda: nope_project(1, 0, 0),
            up,
            lambda: group_n(3),
            lambda: code_n(3),
        ])
        jobs = [
            (lambda m=m, c=c: nope_project(m, 0, c), lambda m=m, c=c: nope_store(m, 0, c))
            for m in range(M_TILES)
            for c in range(2)
        ]
        order = lagged(jobs, 3)[3:]
        spread(order, 19 - done[0])
        kjobs = []
        for m in range(M_TILES):
            kjobs.append((lambda m=m: rot_project(m), lambda m=m: rot_products(m)))
            for c in range(2):
                kjobs.append((lambda m=m, c=c: nope_project(m, 1, c), lambda m=m, c=c: nope_store(m, 1, c)))
            kjobs.append((lambda m=m: pass_project(m), lambda m=m: rope_store(m)))
        vjobs = [
            [(lambda m=m, c=c: value_project(m, c), lambda m=m, c=c: value_store(m, c, "scalar")) for m in range(M_TILES)]
            for c in range(2)
        ]
        spread(lagged(kjobs[:K1], LAG), 22 - done[0])
        spread(lagged(kjobs[K1:K2] + vjobs[0], LAG), 25 - done[0])
        spread(lagged(kjobs[K2:] + vjobs[1], LAG), 28 - done[0])
        for m in range(M_TILES):
            value_project(m, 2)
        for m in range(M_TILES):
            value_store(m, 2, "scalar" if m % 2 == 0 else "vector")
